import numpy as np
import ml_dtypes


def mxq(x, axis, fmt="e4m3"):
    dtype, down = {"e4m3": (ml_dtypes.float8_e4m3fn, 7), "e5m2": (ml_dtypes.float8_e5m2, 14)}[fmt]
    v = np.moveaxis(np.asarray(x, np.float32).astype(ml_dtypes.bfloat16).astype(np.float64), axis, -1)
    blocks = v.reshape(v.shape[:-1] + (-1, 32))
    amax = np.abs(blocks).max(-1, keepdims=True)
    byte = np.maximum(np.where(amax > 0, np.frexp(amax)[1] - 1 + 127, 0) - down, 1)
    scale = np.exp2(byte - 127.0)
    codes = (blocks / scale).astype(np.float32).astype(dtype).astype(np.float64)
    return np.moveaxis((codes * scale).reshape(v.shape), -1, axis)


WIDE = False


def mx_kscale(k):
    if not WIDE:
        return np.ones(k)
    levels = np.array([10, -10, 5, -5, 0])
    a = np.random.permutation(np.resize(levels, k // 512 * 4)).reshape(k // 512, 4)
    idx = np.arange(k)
    return np.exp2(a[idx // 512, idx % 128 // 32])


BF16 = ml_dtypes.bfloat16


def bf(x):
    return np.asarray(x, np.float32).astype(BF16)


def f64(x):
    return np.asarray(x).astype(np.float64)


B, N, P, C, HID, NB, E, MAXLEN = 2, 64, 3, 256, 128, 63, 512, 2056
EPS = 1e-5


def setup_inputs():
    s, t = mx_kscale(E), mx_kscale(E)
    return {"h1": bf(np.maximum(np.random.standard_normal((B, N, N, E)), 0.0) * s),
            "edge_mask": bf(np.random.random((B, N, N)) > 0.15),
            "W2": bf(np.random.standard_normal((E, E)) * 1.4 / np.sqrt(E) / s[:, None] * t),
            "b2": bf(np.random.standard_normal(E) * 0.3 * t),
            "W3": bf(np.random.standard_normal((E, E)) * 1.4 / np.sqrt(E) / t[:, None]),
            "b3": bf(np.random.standard_normal(E) * 0.3),
            "ln_g": bf(1.0 + 0.2 * np.random.standard_normal(E)),
            "ln_b": bf(0.2 * np.random.standard_normal(E))}


def reference(h1, edge_mask, W2, b2, W3, b3, ln_g, ln_b):
    h = np.maximum((mxq(f64(h1), 3, "e4m3") @ mxq(f64(W2), 0, "e4m3")) + f64(b2), 0.0)
    h = (mxq(h, 3, "e4m3") @ mxq(f64(W3), 0, "e4m3")) + f64(b3)
    mu = h.mean(-1, keepdims=True)
    var = h.var(-1, keepdims=True)
    h = (h - mu) / np.sqrt(var + EPS) * f64(ln_g) + f64(ln_b)
    return h * f64(edge_mask)[..., None]

@@ -1,0 +1,228 @@
+from contextlib import ExitStack
+
+import concourse.mybir as mybir
+from concourse.masks import make_identity
+
+F32 = mybir.dt.float32
+BF16 = mybir.dt.bfloat16
+U32 = mybir.dt.uint32
+U8 = mybir.dt.uint8
+FP8X4 = mybir.dt.float8_e4m3fn_x4
+ALU = mybir.AluOpType
+ACT = mybir.ActivationFunctionType
+
+P = 128
+PACK = 4
+E = 512
+ROWS = 2 * 64 * 64
+ROWS_PER_PARTITION = ROWS // P
+TILES_PER_CHUNK = 4
+CHUNK_COLS = TILES_PER_CHUNK * P
+N_CHUNKS = ROWS_PER_PARTITION // TILES_PER_CHUNK
+WORDS = E // 2
+EPS = 1e-5
+
+FLOPS = 2 * 2 * ROWS * E * E
+
+
+def tile_edgefeaturenet_pb_t_kernel(tc, h1, edge_mask, W2, b2, W3, b3, ln_g, ln_b, out):
+    nc = tc.nc
+    h1_rows = h1.flatten_outer_dims().rearrange("(p t) k -> p (t k)", t=ROWS_PER_PARTITION)
+    out_rows = out.flatten_outer_dims().rearrange("(p t) f -> p (t f)", t=ROWS_PER_PARTITION)
+    mask_rows = edge_mask.rearrange("b n m -> (b n m)").rearrange("(p t) -> p t", t=ROWS_PER_PARTITION)
+
+    with ExitStack() as ctx:
+        keep = ctx.enter_context(tc.tile_pool(name="keep", bufs=1))
+        stage = ctx.enter_context(tc.tile_pool(name="stage", bufs=1))
+        loads = ctx.enter_context(tc.tile_pool(name="loads", bufs=3))
+        work = ctx.enter_context(tc.tile_pool(name="work", bufs=2))
+        rowwork = ctx.enter_context(tc.tile_pool(name="rowwork", bufs=4))
+        small = ctx.enter_context(tc.tile_pool(name="small", bufs=3))
+        stores = ctx.enter_context(tc.tile_pool(name="stores", bufs=3))
+        psum_t = ctx.enter_context(tc.psum_pool(name="psum_t", bufs=2))
+        psum_1 = ctx.enter_context(tc.psum_pool(name="psum_1", bufs=3))
+        psum_2 = ctx.enter_context(tc.psum_pool(name="psum_2", bufs=3))
+
+        w2_raw = stage.tile([P, PACK, E], BF16)
+        for u in range(2):
+            nc.sync.dma_start(
+                out=w2_raw[:, 2 * u : 2 * u + 2, :],
+                in_=W2[256 * u : 256 * u + 256, :].rearrange("(q e) n -> q e n", e=2),
+            )
+        w3_raw = stage.tile([P, PACK, E], BF16)
+        nc.scalar.dma_start(out=w3_raw[:], in_=W3.rearrange("(p t) n -> p t n", t=PACK))
+
+        w2_grouped = stage.tile([P, E, PACK], BF16, align_bytes=64)
+        nc.vector.tensor_copy(
+            out=w2_grouped[:].rearrange("q (m r) t -> q m r t", m=PACK),
+            in_=w2_raw[:].rearrange("q t (r m) -> q m r t", m=PACK),
+        )
+        w3_grouped = stage.tile([P, E, PACK], BF16, align_bytes=64)
+        nc.vector.tensor_copy(out=w3_grouped[:], in_=w3_raw[:].rearrange("p t n -> p n t"))
+        w2_codes = keep.tile([P, E], U32, align_bytes=64)
+        w2_scales = keep.tile([P, E], U8, align_bytes=64)
+        nc.vector.quantize_mx(
+            out=w2_codes[:].bitcast(FP8X4),
+            scales=w2_scales[:],
+            in_=w2_grouped[:].rearrange("q n t -> q (n t)"),
+        )
+        w3_codes = keep.tile([P, E], U32, align_bytes=64)
+        w3_scales = keep.tile([P, E], U8, align_bytes=64)
+        nc.vector.quantize_mx(
+            out=w3_codes[:].bitcast(FP8X4),
+            scales=w3_scales[:],
+            in_=w3_grouped[:].rearrange("p n t -> p (n t)"),
+        )
+
+        ident = keep.tile([P, P], F32)
+        make_identity(nc, ident[:])
+        eps = keep.tile([P, 1], F32)
+        nc.vector.memset(eps[:], EPS)
+        b2_bf = keep.tile([P, PACK], BF16)
+        nc.scalar.dma_start(out=b2_bf[:], in_=b2.rearrange("(r m) -> r m", m=PACK))
+        b2_f32 = keep.tile([P, PACK], F32)
+        nc.vector.tensor_copy(out=b2_f32[:], in_=b2_bf[:])
+        mask_bf = keep.tile([P, ROWS_PER_PARTITION], BF16)
+        nc.scalar.dma_start(out=mask_bf[:], in_=mask_rows)
+        mask_f32 = keep.tile([P, ROWS_PER_PARTITION], F32)
+        nc.vector.tensor_copy(out=mask_f32[:], in_=mask_bf[:])
+        b3_all = keep.tile([P, E], BF16)
+        nc.scalar.dma_start(out=b3_all[:], in_=b3.partition_broadcast(P))
+        gain_all = keep.tile([P, E], BF16)
+        nc.scalar.dma_start(out=gain_all[:], in_=ln_g.partition_broadcast(P))
+        shift_all = keep.tile([P, E], BF16)
+        nc.scalar.dma_start(out=shift_all[:], in_=ln_b.partition_broadcast(P))
+
+        for c in range(N_CHUNKS):
+            chunk_cols = slice(c * TILES_PER_CHUNK * E, (c + 1) * TILES_PER_CHUNK * E)
+            x = loads.tile([P, TILES_PER_CHUNK * E], BF16)
+            nc.sync.dma_start(out=x[:], in_=h1_rows[:, chunk_cols])
+
+            masked_shift = work.tile([P, TILES_PER_CHUNK, E], F32)
+            for j in range(TILES_PER_CHUNK):
+                t = c * TILES_PER_CHUNK + j
+                nc.gpsimd.tensor_scalar(
+                    out=masked_shift[:, j, :],
+                    in0=shift_all[:],
+                    scalar1=mask_f32[:, t : t + 1],
+                    scalar2=0.0,
+                    op0=ALU.mult,
+                    op1=ALU.add,
+                )
+
+            x_words = x[:].bitcast(F32)
+            x_grouped = work.tile([P, CHUNK_COLS * PACK], BF16, align_bytes=64)
+            x_grouped_words = x_grouped[:].bitcast(F32).rearrange("q (n u) -> q n u", u=2)
+            for half in range(2):
+                flipped = psum_t.tile([P, 2, 2 * P], F32)
+                for jj in range(2):
+                    j = 2 * half + jj
+                    for u in range(2):
+                        nc.tensor.transpose(
+                            flipped[:, u, jj * P : (jj + 1) * P],
+                            x_words[:, j * WORDS + u * P : j * WORDS + (u + 1) * P],
+                            ident[:],
+                        )
+                nc.scalar.copy(
+                    out=x_grouped_words[:, half * 2 * P : (half + 1) * 2 * P, :],
+                    in_=flipped[:].rearrange("q u n -> q n u"),
+                )
+            x_codes = work.tile([P, CHUNK_COLS], U32, align_bytes=64)
+            x_scales = work.tile([P, CHUNK_COLS], U8, align_bytes=64)
+            nc.vector.quantize_mx(out=x_codes[:].bitcast(FP8X4), scales=x_scales[:], in_=x_grouped[:])
+
+            h_planes = work.tile([P, PACK, CHUNK_COLS], BF16)
+            for m in range(PACK):
+                acc1 = psum_1.tile([P, CHUNK_COLS], F32)
+                nc.tensor.matmul_mx(
+                    out=acc1[:],
+                    lhsT=w2_codes[:, m * P : (m + 1) * P].bitcast(FP8X4),
+                    lhsT_scale=w2_scales[:, m * P : (m + 1) * P],
+                    rhs=x_codes[:].bitcast(FP8X4),
+                    rhs_scale=x_scales[:],
+                    start=True,
+                    stop=True,
+                )
+                nc.scalar.activation(
+                    out=h_planes[:, m, :], in_=acc1[:], func=ACT.Relu, bias=b2_f32[:, m : m + 1], scale=1.0
+                )
+            h_grouped = work.tile([P, CHUNK_COLS, PACK], BF16, align_bytes=64)
+            nc.scalar.copy(
+                out=h_grouped[:].rearrange("p (n i) t -> p n t i", i=4),
+                in_=h_planes[:].rearrange("p t (n i) -> p n t i", i=4),
+            )
+            h_codes = work.tile([P, CHUNK_COLS], U32, align_bytes=64)
+            h_scales = work.tile([P, CHUNK_COLS], U8, align_bytes=64)
+            nc.vector.quantize_mx(
+                out=h_codes[:].bitcast(FP8X4),
+                scales=h_scales[:],
+                in_=h_grouped[:].rearrange("p n t -> p (n t)"),
+            )
+
+            y = work.tile([P, TILES_PER_CHUNK, E], F32)
+            row_sum = small.tile([P, TILES_PER_CHUNK], F32)
+            for j in range(TILES_PER_CHUNK):
+                acc2 = psum_2.tile([P, E], F32)
+                nc.tensor.matmul_mx(
+                    out=acc2[:],
+                    lhsT=h_codes[:, j * P : (j + 1) * P].bitcast(FP8X4),
+                    lhsT_scale=h_scales[:, j * P : (j + 1) * P],
+                    rhs=w3_codes[:].bitcast(FP8X4),
+                    rhs_scale=w3_scales[:],
+                    start=True,
+                    stop=True,
+                )
+                nc.vector.scalar_tensor_tensor(
+                    out=y[:, j, :],
+                    in0=acc2[:],
+                    scalar=1.0,
+                    in1=b3_all[:],
+                    op0=ALU.mult,
+                    op1=ALU.add,
+                    accum_out=row_sum[:, j : j + 1],
+                )
+            neg_mean = small.tile([P, TILES_PER_CHUNK], F32)
+            nc.vector.tensor_scalar(
+                out=neg_mean[:], in0=row_sum[:], scalar1=-1.0 / E, scalar2=None, op0=ALU.mult
+            )
+            square_sum = small.tile([P, TILES_PER_CHUNK], F32)
+            for j in range(TILES_PER_CHUNK):
+                squares = rowwork.tile([P, E], F32)
+                nc.scalar.activation(
+                    out=squares[:],
+                    in_=y[:, j, :],
+                    func=ACT.Square,
+                    bias=neg_mean[:, j : j + 1],
+                    scale=1.0,
+                    accum_out=square_sum[:, j : j + 1],
+                )
+            std = small.tile([P, TILES_PER_CHUNK], F32)
+            nc.scalar.activation(out=std[:], in_=square_sum[:], func=ACT.Sqrt, bias=eps[:, 0:1], scale=1.0 / E)
+            inv_std = small.tile([P, TILES_PER_CHUNK], F32)
+            nc.vector.reciprocal(out=inv_std[:], in_=std[:])
+            row_scale = small.tile([P, TILES_PER_CHUNK], F32)
+            nc.vector.tensor_mul(
+                out=row_scale[:],
+                in0=inv_std[:],
+                in1=mask_f32[:, c * TILES_PER_CHUNK : (c + 1) * TILES_PER_CHUNK],
+            )
+            result = stores.tile([P, TILES_PER_CHUNK, E], F32)
+            for j in range(TILES_PER_CHUNK):
+                gained = rowwork.tile([P, E], F32)
+                nc.vector.scalar_tensor_tensor(
+                    out=gained[:],
+                    in0=y[:, j, :],
+                    scalar=neg_mean[:, j : j + 1],
+                    in1=gain_all[:],
+                    op0=ALU.add,
+                    op1=ALU.mult,
+                )
+                nc.vector.scalar_tensor_tensor(
+                    out=result[:, j, :],
+                    in0=gained[:],
+                    scalar=row_scale[:, j : j + 1],
+                    in1=masked_shift[:, j, :],
+                    op0=ALU.mult,
+                    op1=ALU.add,
+                )
+            nc.sync.dma_start(out=out_rows[:, chunk_cols], in_=result[:].rearrange("p j f -> p (j f)"))

@@ -33,31 +33,238 @@ def tile_edgefeaturenet_pb_t_kernel(tc, h1, edge_mask, W2, b2, W3, b3, ln_g, ln_
 
     with ExitStack() as ctx:
         keep = ctx.enter_context(tc.tile_pool(name="keep", bufs=1))
-        stage = ctx.enter_context(tc.tile_pool(name="stage", bufs=1))
-        loads = ctx.enter_context(tc.tile_pool(name="loads", bufs=3))
-        work = ctx.enter_context(tc.tile_pool(name="work", bufs=2))
-        rowwork = ctx.enter_context(tc.tile_pool(name="rowwork", bufs=4))
-        small = ctx.enter_context(tc.tile_pool(name="small", bufs=3))
-        stores = ctx.enter_context(tc.tile_pool(name="stores", bufs=3))
+        two = ctx.enter_context(tc.tile_pool(name="two", bufs=2))
+        three = ctx.enter_context(tc.tile_pool(name="three", bufs=3))
+        four = ctx.enter_context(tc.tile_pool(name="four", bufs=4))
         psum_t = ctx.enter_context(tc.psum_pool(name="psum_t", bufs=2))
         psum_1 = ctx.enter_context(tc.psum_pool(name="psum_1", bufs=3))
         psum_2 = ctx.enter_context(tc.psum_pool(name="psum_2", bufs=3))
+        ctx.enter_context(tc.manual_schedule())
 
-        w2_raw = stage.tile([P, PACK, E], BF16)
+        live = {}
+
+        def chunk_cols(c):
+            return slice(c * TILES_PER_CHUNK * E, (c + 1) * TILES_PER_CHUNK * E)
+
+        def load(c):
+            x = three.tile([P, TILES_PER_CHUNK * E], BF16, name="x")
+            nc.sync.dma_start(out=x[:], in_=h1_rows[:, chunk_cols(c)])
+            live["x", c] = x
+
+        def mask_the_shift(c):
+            masked_shift = three.tile([P, TILES_PER_CHUNK, E], F32, name="masked_shift")
+            for j in range(TILES_PER_CHUNK):
+                t = c * TILES_PER_CHUNK + j
+                nc.gpsimd.tensor_scalar(
+                    out=masked_shift[:, j, :],
+                    in0=shift_all[:],
+                    scalar1=mask_f32[:, t : t + 1],
+                    scalar2=0.0,
+                    op0=ALU.mult,
+                    op1=ALU.add,
+                )
+            live["masked_shift", c] = masked_shift
+
+        def flip(c):
+            x_words = live["x", c][:].bitcast(F32)
+            for half in range(2):
+                flipped = psum_t.tile([P, 2, 2 * P], F32, name="flipped")
+                for jj in range(2):
+                    j = 2 * half + jj
+                    for u in range(2):
+                        nc.tensor.transpose(
+                            flipped[:, u, jj * P : (jj + 1) * P],
+                            x_words[:, j * WORDS + u * P : j * WORDS + (u + 1) * P],
+                            ident[:],
+                        )
+                live["flipped", c, half] = flipped
+
+        def group_x(c):
+            x_grouped = two.tile([P, CHUNK_COLS * PACK], BF16, align_bytes=64, name="x_grouped")
+            x_grouped_words = x_grouped[:].bitcast(F32).rearrange("q (n u) -> q n u", u=2)
+            for half in range(2):
+                nc.scalar.copy(
+                    out=x_grouped_words[:, half * 2 * P : (half + 1) * 2 * P, :],
+                    in_=live["flipped", c, half][:].rearrange("q u n -> q n u"),
+                )
+            live["x_grouped", c] = x_grouped
+
+        def quantise_x(c):
+            x_codes = four.tile([P, CHUNK_COLS], U32, align_bytes=64, name="x_codes")
+            x_scales = four.tile([P, CHUNK_COLS], U8, align_bytes=64, name="x_scales")
+            nc.vector.quantize_mx(
+                out=x_codes[:].bitcast(FP8X4), scales=x_scales[:], in_=live["x_grouped", c][:]
+            )
+            live["x_codes", c] = x_codes
+            live["x_scales", c] = x_scales
+
+        def layer1_pass(c, m):
+            acc1 = psum_1.tile([P, CHUNK_COLS], F32, name="acc1")
+            nc.tensor.matmul_mx(
+                out=acc1[:],
+                lhsT=w2_codes[:, m * P : (m + 1) * P].bitcast(FP8X4),
+                lhsT_scale=w2_scales[:, m * P : (m + 1) * P],
+                rhs=live["x_codes", c][:].bitcast(FP8X4),
+                rhs_scale=live["x_scales", c][:],
+                start=True,
+                stop=True,
+            )
+            live["acc1", c, m] = acc1
+
+        def relu_and_group_h(c):
+            h_planes = two.tile([P, PACK, CHUNK_COLS], BF16, name="h_planes")
+            for m in range(PACK):
+                nc.scalar.activation(
+                    out=h_planes[:, m, :],
+                    in_=live["acc1", c, m][:],
+                    func=ACT.Relu,
+                    bias=b2_f32[:, m : m + 1],
+                    scale=1.0,
+                )
+            h_grouped = two.tile([P, CHUNK_COLS, PACK], BF16, align_bytes=64, name="h_grouped")
+            nc.scalar.copy(
+                out=h_grouped[:].rearrange("p (n i) t -> p n t i", i=4),
+                in_=h_planes[:].rearrange("p t (n i) -> p n t i", i=4),
+            )
+            live["h_grouped", c] = h_grouped
+
+        def quantise_h(c):
+            h_codes = three.tile([P, CHUNK_COLS], U32, align_bytes=64, name="h_codes")
+            h_scales = three.tile([P, CHUNK_COLS], U8, align_bytes=64, name="h_scales")
+            nc.vector.quantize_mx(
+                out=h_codes[:].bitcast(FP8X4),
+                scales=h_scales[:],
+                in_=live["h_grouped", c][:].rearrange("p n t -> p (n t)"),
+            )
+            live["h_codes", c] = h_codes
+            live["h_scales", c] = h_scales
+
+        def layer2_pass(c, j):
+            acc2 = psum_2.tile([P, E], F32, name="acc2")
+            nc.tensor.matmul_mx(
+                out=acc2[:],
+                lhsT=live["h_codes", c][:, j * P : (j + 1) * P].bitcast(FP8X4),
+                lhsT_scale=live["h_scales", c][:, j * P : (j + 1) * P],
+                rhs=w3_codes[:].bitcast(FP8X4),
+                rhs_scale=w3_scales[:],
+                start=True,
+                stop=True,
+            )
+            live["acc2", c, j] = acc2
+
+        def add_bias_and_mean(c):
+            y = two.tile([P, TILES_PER_CHUNK, E], F32, name="y")
+            row_sum = three.tile([P, TILES_PER_CHUNK], F32, name="row_sum")
+            for j in range(TILES_PER_CHUNK):
+                nc.vector.scalar_tensor_tensor(
+                    out=y[:, j, :],
+                    in0=live["acc2", c, j][:],
+                    scalar=1.0,
+                    in1=b3_all[:],
+                    op0=ALU.mult,
+                    op1=ALU.add,
+                    accum_out=row_sum[:, j : j + 1],
+                )
+            neg_mean = three.tile([P, TILES_PER_CHUNK], F32, name="neg_mean")
+            nc.vector.tensor_scalar(
+                out=neg_mean[:], in0=row_sum[:], scalar1=-1.0 / E, scalar2=None, op0=ALU.mult
+            )
+            live["y", c] = y
+            live["neg_mean", c] = neg_mean
+
+        def deviation(c):
+            square_sum = three.tile([P, TILES_PER_CHUNK], F32, name="square_sum")
+            for j in range(TILES_PER_CHUNK):
+                squares = two.tile([P, E], F32, name="squares")
+                nc.scalar.activation(
+                    out=squares[:],
+                    in_=live["y", c][:, j, :],
+                    func=ACT.Square,
+                    bias=live["neg_mean", c][:, j : j + 1],
+                    scale=1.0,
+                    accum_out=square_sum[:, j : j + 1],
+                )
+            std = three.tile([P, TILES_PER_CHUNK], F32, name="std")
+            nc.scalar.activation(out=std[:], in_=square_sum[:], func=ACT.Sqrt, bias=eps[:, 0:1], scale=1.0 / E)
+            live["std", c] = std
+
+        def centre_and_gain(c):
+            gained = three.tile([P, TILES_PER_CHUNK, E], F32, name="gained")
+            for j in range(TILES_PER_CHUNK):
+                nc.vector.scalar_tensor_tensor(
+                    out=gained[:, j, :],
+                    in0=live["y", c][:, j, :],
+                    scalar=live["neg_mean", c][:, j : j + 1],
+                    in1=gain_all[:],
+                    op0=ALU.add,
+                    op1=ALU.mult,
+                )
+            live["gained", c] = gained
+
+        def scale_shift_store(c):
+            inv_std = three.tile([P, TILES_PER_CHUNK], F32, name="inv_std")
+            nc.vector.reciprocal(out=inv_std[:], in_=live["std", c][:])
+            row_scale = three.tile([P, TILES_PER_CHUNK], F32, name="row_scale")
+            nc.vector.tensor_mul(
+                out=row_scale[:],
+                in0=inv_std[:],
+                in1=mask_f32[:, c * TILES_PER_CHUNK : (c + 1) * TILES_PER_CHUNK],
+            )
+            result = three.tile([P, TILES_PER_CHUNK, E], F32, name="result")
+            for j in range(TILES_PER_CHUNK):
+                nc.vector.scalar_tensor_tensor(
+                    out=result[:, j, :],
+                    in0=live["gained", c][:, j, :],
+                    scalar=row_scale[:, j : j + 1],
+                    in1=live["masked_shift", c][:, j, :],
+                    op0=ALU.mult,
+                    op1=ALU.add,
+                )
+                if j % 2 == 1:
+                    first = (c * TILES_PER_CHUNK + j - 1) * E
+                    nc.sync.dma_start(
+                        out=out_rows[:, first : first + 2 * E],
+                        in_=result[:, j - 1 : j + 1, :].rearrange("p j f -> p (j f)"),
+                    )
+
+        def when_in_range(step, c):
+            if 0 <= c < N_CHUNKS:
+                step(c)
+
+        load(0)
+        load(1)
+        w2_raw = keep.tile([P, PACK, E], BF16)
         for u in range(2):
-            nc.sync.dma_start(
+            nc.scalar.dma_start(
                 out=w2_raw[:, 2 * u : 2 * u + 2, :],
                 in_=W2[256 * u : 256 * u + 256, :].rearrange("(q e) n -> q e n", e=2),
             )
-        w3_raw = stage.tile([P, PACK, E], BF16)
+        w3_raw = keep.tile([P, PACK, E], BF16)
         nc.scalar.dma_start(out=w3_raw[:], in_=W3.rearrange("(p t) n -> p t n", t=PACK))
+        b2_bf = keep.tile([P, PACK], BF16)
+        nc.scalar.dma_start(out=b2_bf[:], in_=b2.rearrange("(r m) -> r m", m=PACK))
+        mask_bf = keep.tile([P, ROWS_PER_PARTITION], BF16)
+        nc.scalar.dma_start(out=mask_bf[:], in_=mask_rows)
+        shift_all = keep.tile([P, E], BF16)
+        nc.scalar.dma_start(out=shift_all[:], in_=ln_b.partition_broadcast(P))
+        b3_all = keep.tile([P, E], BF16)
+        nc.scalar.dma_start(out=b3_all[:], in_=b3.partition_broadcast(P))
+        gain_all = keep.tile([P, E], BF16)
+        nc.scalar.dma_start(out=gain_all[:], in_=ln_g.partition_broadcast(P))
 
-        w2_grouped = stage.tile([P, E, PACK], BF16, align_bytes=64)
+        ident = keep.tile([P, P], F32)
+        make_identity(nc, ident[:])
+        eps = keep.tile([P, 1], F32)
+        nc.vector.memset(eps[:], EPS)
+        table_warmer = keep.tile([P, 1], F32)
+        nc.scalar.activation(out=table_warmer[:], in_=eps[:], func=ACT.Sqrt)
+
+        w2_grouped = keep.tile([P, E, PACK], BF16, align_bytes=64)
         nc.vector.tensor_copy(
             out=w2_grouped[:].rearrange("q (m r) t -> q m r t", m=PACK),
             in_=w2_raw[:].rearrange("q t (r m) -> q m r t", m=PACK),
         )
-        w3_grouped = stage.tile([P, E, PACK], BF16, align_bytes=64)
+        w3_grouped = keep.tile([P, E, PACK], BF16, align_bytes=64)
         nc.vector.tensor_copy(out=w3_grouped[:], in_=w3_raw[:].rearrange("p t n -> p n t"))
         w2_codes = keep.tile([P, E], U32, align_bytes=64)
         w2_scales = keep.tile([P, E], U8, align_bytes=64)
@@ -73,156 +280,25 @@ def tile_edgefeaturenet_pb_t_kernel(tc, h1, edge_mask, W2, b2, W3, b3, ln_g, ln_
             scales=w3_scales[:],
             in_=w3_grouped[:].rearrange("p n t -> p (n t)"),
         )
-
-        ident = keep.tile([P, P], F32)
-        make_identity(nc, ident[:])
-        eps = keep.tile([P, 1], F32)
-        nc.vector.memset(eps[:], EPS)
-        b2_bf = keep.tile([P, PACK], BF16)
-        nc.scalar.dma_start(out=b2_bf[:], in_=b2.rearrange("(r m) -> r m", m=PACK))
         b2_f32 = keep.tile([P, PACK], F32)
         nc.vector.tensor_copy(out=b2_f32[:], in_=b2_bf[:])
-        mask_bf = keep.tile([P, ROWS_PER_PARTITION], BF16)
-        nc.scalar.dma_start(out=mask_bf[:], in_=mask_rows)
         mask_f32 = keep.tile([P, ROWS_PER_PARTITION], F32)
         nc.vector.tensor_copy(out=mask_f32[:], in_=mask_bf[:])
-        b3_all = keep.tile([P, E], BF16)
-        nc.scalar.dma_start(out=b3_all[:], in_=b3.partition_broadcast(P))
-        gain_all = keep.tile([P, E], BF16)
-        nc.scalar.dma_start(out=gain_all[:], in_=ln_g.partition_broadcast(P))
-        shift_all = keep.tile([P, E], BF16)
-        nc.scalar.dma_start(out=shift_all[:], in_=ln_b.partition_broadcast(P))
 
-        for c in range(N_CHUNKS):
-            chunk_cols = slice(c * TILES_PER_CHUNK * E, (c + 1) * TILES_PER_CHUNK * E)
-            x = loads.tile([P, TILES_PER_CHUNK * E], BF16)
-            nc.sync.dma_start(out=x[:], in_=h1_rows[:, chunk_cols])
-
-            masked_shift = work.tile([P, TILES_PER_CHUNK, E], F32)
-            for j in range(TILES_PER_CHUNK):
-                t = c * TILES_PER_CHUNK + j
-                nc.gpsimd.tensor_scalar(
-                    out=masked_shift[:, j, :],
-                    in0=shift_all[:],
-                    scalar1=mask_f32[:, t : t + 1],
-                    scalar2=0.0,
-                    op0=ALU.mult,
-                    op1=ALU.add,
-                )
-
-            x_words = x[:].bitcast(F32)
-            x_grouped = work.tile([P, CHUNK_COLS * PACK], BF16, align_bytes=64)
-            x_grouped_words = x_grouped[:].bitcast(F32).rearrange("q (n u) -> q n u", u=2)
-            for half in range(2):
-                flipped = psum_t.tile([P, 2, 2 * P], F32)
-                for jj in range(2):
-                    j = 2 * half + jj
-                    for u in range(2):
-                        nc.tensor.transpose(
-                            flipped[:, u, jj * P : (jj + 1) * P],
-                            x_words[:, j * WORDS + u * P : j * WORDS + (u + 1) * P],
-                            ident[:],
-                        )
-                nc.scalar.copy(
-                    out=x_grouped_words[:, half * 2 * P : (half + 1) * 2 * P, :],
-                    in_=flipped[:].rearrange("q u n -> q n u"),
-                )
-            x_codes = work.tile([P, CHUNK_COLS], U32, align_bytes=64)
-            x_scales = work.tile([P, CHUNK_COLS], U8, align_bytes=64)
-            nc.vector.quantize_mx(out=x_codes[:].bitcast(FP8X4), scales=x_scales[:], in_=x_grouped[:])
-
-            h_planes = work.tile([P, PACK, CHUNK_COLS], BF16)
-            for m in range(PACK):
-                acc1 = psum_1.tile([P, CHUNK_COLS], F32)
-                nc.tensor.matmul_mx(
-                    out=acc1[:],
-                    lhsT=w2_codes[:, m * P : (m + 1) * P].bitcast(FP8X4),
-                    lhsT_scale=w2_scales[:, m * P : (m + 1) * P],
-                    rhs=x_codes[:].bitcast(FP8X4),
-                    rhs_scale=x_scales[:],
-                    start=True,
-                    stop=True,
-                )
-                nc.scalar.activation(
-                    out=h_planes[:, m, :], in_=acc1[:], func=ACT.Relu, bias=b2_f32[:, m : m + 1], scale=1.0
-                )
-            h_grouped = work.tile([P, CHUNK_COLS, PACK], BF16, align_bytes=64)
-            nc.scalar.copy(
-                out=h_grouped[:].rearrange("p (n i) t -> p n t i", i=4),
-                in_=h_planes[:].rearrange("p t (n i) -> p n t i", i=4),
-            )
-            h_codes = work.tile([P, CHUNK_COLS], U32, align_bytes=64)
-            h_scales = work.tile([P, CHUNK_COLS], U8, align_bytes=64)
-            nc.vector.quantize_mx(
-                out=h_codes[:].bitcast(FP8X4),
-                scales=h_scales[:],
-                in_=h_grouped[:].rearrange("p n t -> p (n t)"),
-            )
-
-            y = work.tile([P, TILES_PER_CHUNK, E], F32)
-            row_sum = small.tile([P, TILES_PER_CHUNK], F32)
-            for j in range(TILES_PER_CHUNK):
-                acc2 = psum_2.tile([P, E], F32)
-                nc.tensor.matmul_mx(
-                    out=acc2[:],
-                    lhsT=h_codes[:, j * P : (j + 1) * P].bitcast(FP8X4),
-                    lhsT_scale=h_scales[:, j * P : (j + 1) * P],
-                    rhs=w3_codes[:].bitcast(FP8X4),
-                    rhs_scale=w3_scales[:],
-                    start=True,
-                    stop=True,
-                )
-                nc.vector.scalar_tensor_tensor(
-                    out=y[:, j, :],
-                    in0=acc2[:],
-                    scalar=1.0,
-                    in1=b3_all[:],
-                    op0=ALU.mult,
-                    op1=ALU.add,
-                    accum_out=row_sum[:, j : j + 1],
-                )
-            neg_mean = small.tile([P, TILES_PER_CHUNK], F32)
-            nc.vector.tensor_scalar(
-                out=neg_mean[:], in0=row_sum[:], scalar1=-1.0 / E, scalar2=None, op0=ALU.mult
-            )
-            square_sum = small.tile([P, TILES_PER_CHUNK], F32)
-            for j in range(TILES_PER_CHUNK):
-                squares = rowwork.tile([P, E], F32)
-                nc.scalar.activation(
-                    out=squares[:],
-                    in_=y[:, j, :],
-                    func=ACT.Square,
-                    bias=neg_mean[:, j : j + 1],
-                    scale=1.0,
-                    accum_out=square_sum[:, j : j + 1],
-                )
-            std = small.tile([P, TILES_PER_CHUNK], F32)
-            nc.scalar.activation(out=std[:], in_=square_sum[:], func=ACT.Sqrt, bias=eps[:, 0:1], scale=1.0 / E)
-            inv_std = small.tile([P, TILES_PER_CHUNK], F32)
-            nc.vector.reciprocal(out=inv_std[:], in_=std[:])
-            row_scale = small.tile([P, TILES_PER_CHUNK], F32)
-            nc.vector.tensor_mul(
-                out=row_scale[:],
-                in0=inv_std[:],
-                in1=mask_f32[:, c * TILES_PER_CHUNK : (c + 1) * TILES_PER_CHUNK],
-            )
-            result = stores.tile([P, TILES_PER_CHUNK, E], F32)
-            for j in range(TILES_PER_CHUNK):
-                gained = rowwork.tile([P, E], F32)
-                nc.vector.scalar_tensor_tensor(
-                    out=gained[:],
-                    in0=y[:, j, :],
-                    scalar=neg_mean[:, j : j + 1],
-                    in1=gain_all[:],
-                    op0=ALU.add,
-                    op1=ALU.mult,
-                )
-                nc.vector.scalar_tensor_tensor(
-                    out=result[:, j, :],
-                    in0=gained[:],
-                    scalar=row_scale[:, j : j + 1],
-                    in1=masked_shift[:, j, :],
-                    op0=ALU.mult,
-                    op1=ALU.add,
-                )
-            nc.sync.dma_start(out=out_rows[:, chunk_cols], in_=result[:].rearrange("p j f -> p (j f)"))
+        for i in range(-3, N_CHUNKS + 1):
+            when_in_range(add_bias_and_mean, i)
+            when_in_range(scale_shift_store, i - 1)
+            when_in_range(relu_and_group_h, i + 1)
+            when_in_range(quantise_h, i + 1)
+            when_in_range(flip, i + 3)
+            when_in_range(group_x, i + 3)
+            when_in_range(deviation, i)
+            when_in_range(centre_and_gain, i)
+            when_in_range(quantise_x, i + 3)
+            for q in range(PACK):
+                if 0 <= i + 1 < N_CHUNKS:
+                    layer2_pass(i + 1, q)
+                if 0 <= i + 2 < N_CHUNKS:
+                    layer1_pass(i + 2, q)
+            when_in_range(mask_the_shift, i + 2)
+            when_in_range(load, i + 5)

@@ -37,7 +37,8 @@ def tile_edgefeaturenet_pb_t_kernel(tc, h1, edge_mask, W2, b2, W3, b3, ln_g, ln_
         three = ctx.enter_context(tc.tile_pool(name="three", bufs=3))
         four = ctx.enter_context(tc.tile_pool(name="four", bufs=4))
         psum_t = ctx.enter_context(tc.psum_pool(name="psum_t", bufs=2))
-        psum_1 = ctx.enter_context(tc.psum_pool(name="psum_1", bufs=3))
+        psum_1 = ctx.enter_context(tc.psum_pool(name="psum_1", bufs=2))
+        psum_keep = ctx.enter_context(tc.psum_pool(name="psum_keep", bufs=1))
         psum_2 = ctx.enter_context(tc.psum_pool(name="psum_2", bufs=3))
         ctx.enter_context(tc.manual_schedule())
 
@@ -249,8 +250,13 @@ def tile_edgefeaturenet_pb_t_kernel(tc, h1, edge_mask, W2, b2, W3, b3, ln_g, ln_
         nc.scalar.dma_start(out=shift_all[:], in_=ln_b.partition_broadcast(P))
         b3_all = keep.tile([P, E], BF16)
         nc.scalar.dma_start(out=b3_all[:], in_=b3.partition_broadcast(P))
-        gain_all = keep.tile([P, E], BF16)
-        nc.scalar.dma_start(out=gain_all[:], in_=ln_g.partition_broadcast(P))
+        ones = keep.tile([P, P], BF16)
+        nc.vector.memset(ones[:], 1.0)
+        gain_row = keep.tile([P, E], BF16)
+        nc.vector.memset(gain_row[:], 0.0)
+        nc.scalar.dma_start(out=gain_row[0:1, :], in_=ln_g.rearrange("(o f) -> o f", o=1))
+        gain_all = psum_keep.tile([P, E], F32)
+        nc.tensor.matmul(out=gain_all[:], lhsT=ones[:], rhs=gain_row[:], start=True, stop=True)
 
         ident = keep.tile([P, P], F32)
         make_identity(nc, ident[:])

@@ -112,7 +112,7 @@ def tile_edgefeaturenet_pb_t_kernel(tc, h1, edge_mask, W2, b2, W3, b3, ln_g, ln_
             )
             live["acc1", c, m] = acc1
 
-        def relu_and_group_h(c):
+        def bias_and_relu(c):
             h_planes = two.tile([P, PACK, CHUNK_COLS], BF16, name="h_planes")
             for m in range(PACK):
                 nc.scalar.activation(
@@ -122,10 +122,17 @@ def tile_edgefeaturenet_pb_t_kernel(tc, h1, edge_mask, W2, b2, W3, b3, ln_g, ln_
                     bias=b2_f32[:, m : m + 1],
                     scale=1.0,
                 )
+            live["h_planes", c] = h_planes
+
+        def group_h(c):
             h_grouped = two.tile([P, CHUNK_COLS, PACK], BF16, align_bytes=64, name="h_grouped")
-            nc.scalar.copy(
-                out=h_grouped[:].rearrange("p (n i) t -> p n t i", i=4),
-                in_=h_planes[:].rearrange("p t (n i) -> p n t i", i=4),
+            nc.gpsimd.tensor_scalar(
+                out=h_grouped[:],
+                in0=live["h_planes", c][:].rearrange("p t n -> p n t"),
+                scalar1=1.0,
+                scalar2=0.0,
+                op0=ALU.mult,
+                op1=ALU.add,
             )
             live["h_grouped", c] = h_grouped
 
@@ -232,6 +239,13 @@ def tile_edgefeaturenet_pb_t_kernel(tc, h1, edge_mask, W2, b2, W3, b3, ln_g, ln_
             if 0 <= c < N_CHUNKS:
                 step(c)
 
+        ones = keep.tile([P, P], BF16)
+        nc.vector.memset(ones[:], 1.0)
+        gain_row = keep.tile([P, E], BF16)
+        nc.vector.memset(gain_row[:], 0.0)
+        nc.scalar.dma_start(out=gain_row[0:1, :], in_=ln_g.rearrange("(o f) -> o f", o=1))
+        gain_all = psum_keep.tile([P, E], F32)
+        nc.tensor.matmul(out=gain_all[:], lhsT=ones[:], rhs=gain_row[:], start=True, stop=True)
         load(0)
         load(1)
         w2_raw = keep.tile([P, PACK, E], BF16)
@@ -250,13 +264,6 @@ def tile_edgefeaturenet_pb_t_kernel(tc, h1, edge_mask, W2, b2, W3, b3, ln_g, ln_
         nc.scalar.dma_start(out=shift_all[:], in_=ln_b.partition_broadcast(P))
         b3_all = keep.tile([P, E], BF16)
         nc.scalar.dma_start(out=b3_all[:], in_=b3.partition_broadcast(P))
-        ones = keep.tile([P, P], BF16)
-        nc.vector.memset(ones[:], 1.0)
-        gain_row = keep.tile([P, E], BF16)
-        nc.vector.memset(gain_row[:], 0.0)
-        nc.scalar.dma_start(out=gain_row[0:1, :], in_=ln_g.rearrange("(o f) -> o f", o=1))
-        gain_all = psum_keep.tile([P, E], F32)
-        nc.tensor.matmul(out=gain_all[:], lhsT=ones[:], rhs=gain_row[:], start=True, stop=True)
 
         ident = keep.tile([P, P], F32)
         make_identity(nc, ident[:])
@@ -294,12 +301,13 @@ def tile_edgefeaturenet_pb_t_kernel(tc, h1, edge_mask, W2, b2, W3, b3, ln_g, ln_
         for i in range(-3, N_CHUNKS + 1):
             when_in_range(add_bias_and_mean, i)
             when_in_range(scale_shift_store, i - 1)
-            when_in_range(relu_and_group_h, i + 1)
-            when_in_range(quantise_h, i + 1)
+            when_in_range(bias_and_relu, i + 1)
+            when_in_range(group_h, i + 1)
             when_in_range(flip, i + 3)
             when_in_range(group_x, i + 3)
             when_in_range(deviation, i)
             when_in_range(centre_and_gain, i)
+            when_in_range(quantise_h, i + 1)
             when_in_range(quantise_x, i + 3)
             for q in range(PACK):
                 if 0 <= i + 1 < N_CHUNKS:

from contextlib import ExitStack

import concourse.mybir as mybir
from concourse.masks import make_identity

F32 = mybir.dt.float32
BF16 = mybir.dt.bfloat16
U32 = mybir.dt.uint32
U8 = mybir.dt.uint8
FP8X4 = mybir.dt.float8_e4m3fn_x4
ALU = mybir.AluOpType
ACT = mybir.ActivationFunctionType

P = 128
PACK = 4
E = 512
ROWS = 2 * 64 * 64
ROWS_PER_PARTITION = ROWS // P
TILES_PER_CHUNK = 4
CHUNK_COLS = TILES_PER_CHUNK * P
N_CHUNKS = ROWS_PER_PARTITION // TILES_PER_CHUNK
WORDS = E // 2
EPS = 1e-5

FLOPS = 2 * 2 * ROWS * E * E


def tile_edgefeaturenet_pb_t_kernel(tc, h1, edge_mask, W2, b2, W3, b3, ln_g, ln_b, out):
    nc = tc.nc
    h1_rows = h1.flatten_outer_dims().rearrange("(p t) k -> p (t k)", t=ROWS_PER_PARTITION)
    out_rows = out.flatten_outer_dims().rearrange("(p t) f -> p (t f)", t=ROWS_PER_PARTITION)
    mask_rows = edge_mask.rearrange("b n m -> (b n m)").rearrange("(p t) -> p t", t=ROWS_PER_PARTITION)

    with ExitStack() as ctx:
        keep = ctx.enter_context(tc.tile_pool(name="keep", bufs=1))
        two = ctx.enter_context(tc.tile_pool(name="two", bufs=2))
        three = ctx.enter_context(tc.tile_pool(name="three", bufs=3))
        four = ctx.enter_context(tc.tile_pool(name="four", bufs=4))
        psum_t = ctx.enter_context(tc.psum_pool(name="psum_t", bufs=2))
        psum_1 = ctx.enter_context(tc.psum_pool(name="psum_1", bufs=2))
        psum_keep = ctx.enter_context(tc.psum_pool(name="psum_keep", bufs=1))
        psum_2 = ctx.enter_context(tc.psum_pool(name="psum_2", bufs=3))
        ctx.enter_context(tc.manual_schedule())

        live = {}

        def chunk_cols(c):
            return slice(c * TILES_PER_CHUNK * E, (c + 1) * TILES_PER_CHUNK * E)

        def load(c):
            x = three.tile([P, TILES_PER_CHUNK * E], BF16, name="x")
            nc.sync.dma_start(out=x[:], in_=h1_rows[:, chunk_cols(c)])
            live["x", c] = x

        def mask_the_shift(c):
            masked_shift = three.tile([P, TILES_PER_CHUNK, E], F32, name="masked_shift")
            for j in range(TILES_PER_CHUNK):
                t = c * TILES_PER_CHUNK + j
                nc.gpsimd.tensor_scalar(
                    out=masked_shift[:, j, :],
                    in0=shift_all[:],
                    scalar1=mask_f32[:, t : t + 1],
                    scalar2=0.0,
                    op0=ALU.mult,
                    op1=ALU.add,
                )
            live["masked_shift", c] = masked_shift

        def flip(c):
            x_words = live["x", c][:].bitcast(F32)
            for half in range(2):
                flipped = psum_t.tile([P, 2, 2 * P], F32, name="flipped")
                for jj in range(2):
                    j = 2 * half + jj
                    for u in range(2):
                        nc.tensor.transpose(
                            flipped[:, u, jj * P : (jj + 1) * P],
                            x_words[:, j * WORDS + u * P : j * WORDS + (u + 1) * P],
                            ident[:],
                        )
                live["flipped", c, half] = flipped

        def group_x(c):
            x_grouped = two.tile([P, CHUNK_COLS * PACK], BF16, align_bytes=64, name="x_grouped")
            x_grouped_words = x_grouped[:].bitcast(F32).rearrange("q (n u) -> q n u", u=2)
            for half in range(2):
                nc.scalar.copy(
                    out=x_grouped_words[:, half * 2 * P : (half + 1) * 2 * P, :],
                    in_=live["flipped", c, half][:].rearrange("q u n -> q n u"),
                )
            live["x_grouped", c] = x_grouped

        def quantise_x(c):
            x_codes = four.tile([P, CHUNK_COLS], U32, align_bytes=64, name="x_codes")
            x_scales = four.tile([P, CHUNK_COLS], U8, align_bytes=64, name="x_scales")
            nc.vector.quantize_mx(
                out=x_codes[:].bitcast(FP8X4), scales=x_scales[:], in_=live["x_grouped", c][:]
            )
            live["x_codes", c] = x_codes
            live["x_scales", c] = x_scales

        def layer1_pass(c, m):
            acc1 = psum_1.tile([P, CHUNK_COLS], F32, name="acc1")
            nc.tensor.matmul_mx(
                out=acc1[:],
                lhsT=w2_codes[:, m * P : (m + 1) * P].bitcast(FP8X4),
                lhsT_scale=w2_scales[:, m * P : (m + 1) * P],
                rhs=live["x_codes", c][:].bitcast(FP8X4),
                rhs_scale=live["x_scales", c][:],
                start=True,
                stop=True,
            )
            live["acc1", c, m] = acc1

        def bias_and_relu(c):
            h_planes = two.tile([P, PACK, CHUNK_COLS], BF16, name="h_planes")
            for m in range(PACK):
                nc.scalar.activation(
                    out=h_planes[:, m, :],
                    in_=live["acc1", c, m][:],
                    func=ACT.Relu,
                    bias=b2_f32[:, m : m + 1],
                    scale=1.0,
                )
            live["h_planes", c] = h_planes

        def group_h(c):
            h_grouped = two.tile([P, CHUNK_COLS, PACK], BF16, align_bytes=64, name="h_grouped")
            nc.gpsimd.tensor_scalar(
                out=h_grouped[:],
                in0=live["h_planes", c][:].rearrange("p t n -> p n t"),
                scalar1=1.0,
                scalar2=0.0,
                op0=ALU.mult,
                op1=ALU.add,
            )
            live["h_grouped", c] = h_grouped

        def quantise_h(c):
            h_codes = three.tile([P, CHUNK_COLS], U32, align_bytes=64, name="h_codes")
            h_scales = three.tile([P, CHUNK_COLS], U8, align_bytes=64, name="h_scales")
            nc.vector.quantize_mx(
                out=h_codes[:].bitcast(FP8X4),
                scales=h_scales[:],
                in_=live["h_grouped", c][:].rearrange("p n t -> p (n t)"),
            )
            live["h_codes", c] = h_codes
            live["h_scales", c] = h_scales

        def layer2_pass(c, j):
            acc2 = psum_2.tile([P, E], F32, name="acc2")
            nc.tensor.matmul_mx(
                out=acc2[:],
                lhsT=live["h_codes", c][:, j * P : (j + 1) * P].bitcast(FP8X4),
                lhsT_scale=live["h_scales", c][:, j * P : (j + 1) * P],
                rhs=w3_codes[:].bitcast(FP8X4),
                rhs_scale=w3_scales[:],
                start=True,
                stop=True,
            )
            live["acc2", c, j] = acc2

        def add_bias_and_mean(c):
            y = two.tile([P, TILES_PER_CHUNK, E], F32, name="y")
            row_sum = three.tile([P, TILES_PER_CHUNK], F32, name="row_sum")
            for j in range(TILES_PER_CHUNK):
                nc.vector.scalar_tensor_tensor(
                    out=y[:, j, :],
                    in0=live["acc2", c, j][:],
                    scalar=1.0,
                    in1=b3_all[:],
                    op0=ALU.mult,
                    op1=ALU.add,
                    accum_out=row_sum[:, j : j + 1],
                )
            neg_mean = three.tile([P, TILES_PER_CHUNK], F32, name="neg_mean")
            nc.vector.tensor_scalar(
                out=neg_mean[:], in0=row_sum[:], scalar1=-1.0 / E, scalar2=None, op0=ALU.mult
            )
            live["y", c] = y
            live["neg_mean", c] = neg_mean

        def deviation(c):
            square_sum = three.tile([P, TILES_PER_CHUNK], F32, name="square_sum")
            for j in range(TILES_PER_CHUNK):
                squares = two.tile([P, E], F32, name="squares")
                nc.scalar.activation(
                    out=squares[:],
                    in_=live["y", c][:, j, :],
                    func=ACT.Square,
                    bias=live["neg_mean", c][:, j : j + 1],
                    scale=1.0,
                    accum_out=square_sum[:, j : j + 1],
                )
            std = three.tile([P, TILES_PER_CHUNK], F32, name="std")
            nc.scalar.activation(out=std[:], in_=square_sum[:], func=ACT.Sqrt, bias=eps[:, 0:1], scale=1.0 / E)
            live["std", c] = std

        def centre_and_gain(c):
            gained = three.tile([P, TILES_PER_CHUNK, E], F32, name="gained")
            for j in range(TILES_PER_CHUNK):
                nc.vector.scalar_tensor_tensor(
                    out=gained[:, j, :],
                    in0=live["y", c][:, j, :],
                    scalar=live["neg_mean", c][:, j : j + 1],
                    in1=gain_all[:],
                    op0=ALU.add,
                    op1=ALU.mult,
                )
            live["gained", c] = gained

        def scale_shift_store(c):
            inv_std = three.tile([P, TILES_PER_CHUNK], F32, name="inv_std")
            nc.vector.reciprocal(out=inv_std[:], in_=live["std", c][:])
            row_scale = three.tile([P, TILES_PER_CHUNK], F32, name="row_scale")
            nc.vector.tensor_mul(
                out=row_scale[:],
                in0=inv_std[:],
                in1=mask_f32[:, c * TILES_PER_CHUNK : (c + 1) * TILES_PER_CHUNK],
            )
            result = three.tile([P, TILES_PER_CHUNK, E], F32, name="result")
            for j in range(TILES_PER_CHUNK):
                nc.vector.scalar_tensor_tensor(
                    out=result[:, j, :],
                    in0=live["gained", c][:, j, :],
                    scalar=row_scale[:, j : j + 1],
                    in1=live["masked_shift", c][:, j, :],
                    op0=ALU.mult,
                    op1=ALU.add,
                )
                if j % 2 == 1:
                    first = (c * TILES_PER_CHUNK + j - 1) * E
                    nc.sync.dma_start(
                        out=out_rows[:, first : first + 2 * E],
                        in_=result[:, j - 1 : j + 1, :].rearrange("p j f -> p (j f)"),
                    )

        def when_in_range(step, c):
            if 0 <= c < N_CHUNKS:
                step(c)

        ones = keep.tile([P, P], BF16)
        nc.vector.memset(ones[:], 1.0)
        gain_row = keep.tile([P, E], BF16)
        nc.vector.memset(gain_row[:], 0.0)
        nc.scalar.dma_start(out=gain_row[0:1, :], in_=ln_g.rearrange("(o f) -> o f", o=1))
        gain_all = psum_keep.tile([P, E], F32)
        nc.tensor.matmul(out=gain_all[:], lhsT=ones[:], rhs=gain_row[:], start=True, stop=True)
        load(0)
        load(1)
        w2_raw = keep.tile([P, PACK, E], BF16)
        for u in range(2):
            nc.scalar.dma_start(
                out=w2_raw[:, 2 * u : 2 * u + 2, :],
                in_=W2[256 * u : 256 * u + 256, :].rearrange("(q e) n -> q e n", e=2),
            )
        w3_raw = keep.tile([P, PACK, E], BF16)
        nc.scalar.dma_start(out=w3_raw[:], in_=W3.rearrange("(p t) n -> p t n", t=PACK))
        b2_bf = keep.tile([P, PACK], BF16)
        nc.scalar.dma_start(out=b2_bf[:], in_=b2.rearrange("(r m) -> r m", m=PACK))
        mask_bf = keep.tile([P, ROWS_PER_PARTITION], BF16)
        nc.scalar.dma_start(out=mask_bf[:], in_=mask_rows)
        shift_all = keep.tile([P, E], BF16)
        nc.scalar.dma_start(out=shift_all[:], in_=ln_b.partition_broadcast(P))
        b3_all = keep.tile([P, E], BF16)
        nc.scalar.dma_start(out=b3_all[:], in_=b3.partition_broadcast(P))

        ident = keep.tile([P, P], F32)
        make_identity(nc, ident[:])
        eps = keep.tile([P, 1], F32)
        nc.vector.memset(eps[:], EPS)
        table_warmer = keep.tile([P, 1], F32)
        nc.scalar.activation(out=table_warmer[:], in_=eps[:], func=ACT.Sqrt)

        w2_grouped = keep.tile([P, E, PACK], BF16, align_bytes=64)
        nc.vector.tensor_copy(
            out=w2_grouped[:].rearrange("q (m r) t -> q m r t", m=PACK),
            in_=w2_raw[:].rearrange("q t (r m) -> q m r t", m=PACK),
        )
        w3_grouped = keep.tile([P, E, PACK], BF16, align_bytes=64)
        nc.vector.tensor_copy(out=w3_grouped[:], in_=w3_raw[:].rearrange("p t n -> p n t"))
        w2_codes = keep.tile([P, E], U32, align_bytes=64)
        w2_scales = keep.tile([P, E], U8, align_bytes=64)
        nc.vector.quantize_mx(
            out=w2_codes[:].bitcast(FP8X4),
            scales=w2_scales[:],
            in_=w2_grouped[:].rearrange("q n t -> q (n t)"),
        )
        w3_codes = keep.tile([P, E], U32, align_bytes=64)
        w3_scales = keep.tile([P, E], U8, align_bytes=64)
        nc.vector.quantize_mx(
            out=w3_codes[:].bitcast(FP8X4),
            scales=w3_scales[:],
            in_=w3_grouped[:].rearrange("p n t -> p (n t)"),
        )
        b2_f32 = keep.tile([P, PACK], F32)
        nc.vector.tensor_copy(out=b2_f32[:], in_=b2_bf[:])
        mask_f32 = keep.tile([P, ROWS_PER_PARTITION], F32)
        nc.vector.tensor_copy(out=mask_f32[:], in_=mask_bf[:])

        for i in range(-3, N_CHUNKS + 1):
            when_in_range(add_bias_and_mean, i)
            when_in_range(scale_shift_store, i - 1)
            when_in_range(bias_and_relu, i + 1)
            when_in_range(group_h, i + 1)
            when_in_range(flip, i + 3)
            when_in_range(group_x, i + 3)
            when_in_range(deviation, i)
            when_in_range(centre_and_gain, i)
            when_in_range(quantise_h, i + 1)
            when_in_range(quantise_x, i + 3)
            for q in range(PACK):
                if 0 <= i + 1 < N_CHUNKS:
                    layer2_pass(i + 1, q)
                if 0 <= i + 2 < N_CHUNKS:
                    layer1_pass(i + 2, q)
            when_in_range(mask_the_shift, i + 2)
            when_in_range(load, i + 5)
